import numpy as np
import ml_dtypes


def mxq(x, axis, fmt="e4m3"):
    dtype, down = {"e4m3": (ml_dtypes.float8_e4m3fn, 7), "e5m2": (ml_dtypes.float8_e5m2, 14)}[fmt]
    v = np.moveaxis(np.asarray(x, np.float32).astype(ml_dtypes.bfloat16).astype(np.float64), axis, -1)
    blocks = v.reshape(v.shape[:-1] + (-1, 32))
    amax = np.abs(blocks).max(-1, keepdims=True)
    byte = np.maximum(np.where(amax > 0, np.frexp(amax)[1] - 1 + 127, 0) - down, 1)
    scale = np.exp2(byte - 127.0)
    codes = (blocks / scale).astype(np.float32).astype(dtype).astype(np.float64)
    return np.moveaxis((codes * scale).reshape(v.shape), -1, axis)


WIDE = False


def mx_kscale(k):
    if not WIDE:
        return np.ones(k)
    levels = np.array([20, -20, 10, -10, 0])
    a = np.random.permutation(np.resize(levels, k // 512 * 4)).reshape(k // 512, 4)
    idx = np.arange(k)
    return np.exp2(a[idx // 512, idx % 128 // 32])


BF16 = ml_dtypes.bfloat16


def bf(x):
    return np.asarray(x, np.float32).astype(BF16)


def f64(x):
    return np.asarray(x).astype(np.float64)


E, LMAX, MMAX, CIN, COUT = 2048, 2, 2, 128, 512
NS = [LMAX + 1 - m for m in range(MMAX + 1)]
NC = NS[0] + sum(2 * n for n in NS[1:])


def setup_inputs():
    us = [mx_kscale(n * COUT) for n in NS]
    sg = np.concatenate([us[0].reshape(NS[0], COUT)] + [np.tile(us[m].reshape(NS[m], COUT), (2, 1)) for m in range(1, MMAX + 1)], axis=0)
    x = np.random.standard_normal((E, NC, CIN))
    W0 = np.random.standard_normal((NS[0] * COUT, NS[0] * CIN)) / np.sqrt(NS[0] * CIN) / us[0][:, None]
    b0 = np.random.standard_normal(NS[0] * COUT) * 0.3
    W1 = np.random.standard_normal((2 * NS[1] * COUT, NS[1] * CIN)) / (np.sqrt(2.0) * np.sqrt(NS[1] * CIN)) / np.tile(us[1], 2)[:, None]
    W2 = np.random.standard_normal((2 * NS[2] * COUT, NS[2] * CIN)) / (np.sqrt(2.0) * np.sqrt(NS[2] * CIN)) / np.tile(us[2], 2)[:, None]
    g = np.random.standard_normal((E, NC, COUT)) * np.exp2(np.random.randint(-12, 1, (E, 1, 1))) * 16.0 * sg
    return {"x": bf(x), "W0": bf(W0), "b0": bf(b0), "W1": bf(W1), "W2": bf(W2), "grad_out": bf(g)}


def reference(x, W0, b0, W1, W2, grad_out):
    g = f64(grad_out)
    Wm = [f64(W1), f64(W2)]
    outs = []
    g0 = g[:, :NS[0]].reshape(E, NS[0] * COUT)
    gx0 = mxq(g0, 1, "e5m2") @ mxq(f64(W0), 0, "e4m3")
    outs.append(gx0.reshape(E, NS[0], CIN))
    offset = NS[0]
    for m in range(1, MMAX + 1):
        n = NS[m]
        of = n * COUT
        gp = mxq(g[:, offset:offset + n].reshape(E, of), 1, "e5m2")
        gn = mxq(g[:, offset + n:offset + 2 * n].reshape(E, of), 1, "e5m2")
        offset += 2 * n
        Wr = mxq(Wm[m - 1][:of], 0, "e4m3")
        Wi = mxq(Wm[m - 1][of:], 0, "e4m3")
        gr = (gp @ Wr) + (gn @ Wi)
        gi = (gn @ Wr) - (gp @ Wi)
        outs.append(gr.reshape(E, n, CIN))
        outs.append(gi.reshape(E, n, CIN))
    return np.concatenate(outs, axis=1)

@@ -1,0 +1,278 @@
+import concourse.mybir as mybir
+from concourse.masks import make_identity
+
+F32 = mybir.dt.float32
+BF16 = mybir.dt.bfloat16
+U32 = mybir.dt.uint32
+U8 = mybir.dt.uint8
+I32 = mybir.dt.int32
+E4X4 = mybir.dt.float8_e4m3fn_x4
+E5X4 = mybir.dt.float8_e5m2_x4
+
+P = 128
+NT = 16
+KP = 512
+WPP = KP // 2
+CIN = 128
+OUTW = 9 * CIN
+RING = 7
+
+FLOPS = 2 * 2048 * (1536 * 384 + 4 * 1024 * 256 + 4 * 512 * 128)
+BYTES = 2048 * 9 * 512 * 2 + (1536 * 384 + 2048 * 256 + 1024 * 128) * 2 + 2048 * 9 * 128 * 4
+
+PINNED = True
+
+
+def make_units():
+    units = []
+    t = 0
+    for size in (1, 1, 2, 4, 4, 4):
+        units.append(("m2", 7, 2, t, size))
+        t += size
+    for t in range(0, NT, 2):
+        units.append(("m0", 0, 3, t, 2))
+    for t in range(0, NT, 2):
+        units.append(("m1", 3, 4, t, 2))
+    return units
+
+
+def tile_so2linear_t_kernel(tc, x, W0, b0, W1, W2, grad_out, out):
+    if PINNED:
+        with tc.manual_schedule():
+            body(tc, W0, W1, W2, grad_out, out)
+    else:
+        body(tc, W0, W1, W2, grad_out, out)
+
+
+def body(tc, W0, W1, W2, grad_out, out):
+    nc = tc.nc
+    gv = grad_out.rearrange("(p t) c k -> p t (c k)", t=NT)
+    ov = out.rearrange("(p t) c k -> p t (c k)", t=NT)
+    units = make_units()
+    n = len(units)
+
+    with tc.tile_pool(name="const", bufs=1) as const, tc.tile_pool(name="wtmp", bufs=1) as wtmp, tc.tile_pool(
+        name="ring", bufs=RING
+    ) as ring, tc.tile_pool(name="stage", bufs=3) as stage, tc.tile_pool(name="outs", bufs=1) as outs, tc.psum_pool(
+        name="psum", bufs=4
+    ) as psum:
+        ident = const.tile([P, P], F32, name="ident")
+        make_identity(nc, ident[:])
+
+        w0c = const.tile([P, 1280], U32, name="w0c", align_bytes=64)
+        w0s = const.tile([P, 1280], U8, name="w0s", align_bytes=64)
+        w1c = const.tile([P, 1536], U32, name="w1c", align_bytes=64)
+        w1s = const.tile([P, 1536], U8, name="w1s", align_bytes=64)
+        w2c = const.tile([P, 640], U32, name="w2c", align_bytes=64)
+        w2s = const.tile([P, 640], U8, name="w2s", align_bytes=64)
+        raw0 = wtmp.tile([P, 12, 384], BF16, name="raw0")
+        raw1 = wtmp.tile([P, 16, 256], BF16, name="raw1")
+        raw2 = wtmp.tile([P, 8, 128], BF16, name="raw2")
+
+        def load_w(raw, w):
+            nc.sync.dma_start(
+                out=raw[:].rearrange("p (a e) c -> p a (e c)", e=2),
+                in_=w.rearrange("(a p e) c -> p a (e c)", p=P, e=2),
+            )
+
+        def regroup(dst, src, negate):
+            d = dst.rearrange("p (c i) t -> p c t i", i=4)
+            s = src.rearrange("p t (c i) -> p c t i", i=4)
+            if negate:
+                nc.vector.tensor_scalar_mul(out=d, in0=s, scalar1=-1.0)
+            else:
+                nc.vector.tensor_copy(out=d, in_=s)
+
+        def quant_w(codes, scales, grouped, lo, hi):
+            nc.vector.quantize_mx(
+                out=codes[:, lo:hi].bitcast(E4X4),
+                scales=scales[:, lo:hi],
+                in_=grouped[:, lo:hi, :].rearrange("p c t -> p (c t)"),
+            )
+
+        def zero(codes, scales, lo, hi):
+            nc.vector.memset(codes[:, lo:hi].bitcast(I32), 0)
+            nc.vector.memset(scales[:, lo:hi].bitcast(I32), 0)
+
+        wgrp = {}
+
+        def prep_w2():
+            gw = wtmp.tile([P, 384, 4], BF16, name="gw2", tag="gw", align_bytes=64)
+            regroup(gw[:, 0:128, :], raw2[:, 4:8, :], False)
+            regroup(gw[:, 128:256, :], raw2[:, 0:4, :], False)
+            regroup(gw[:, 256:384, :], raw2[:, 4:8, :], True)
+            quant_w(w2c, w2s, gw, 0, 256)
+            quant_w(w2c, w2s, gw, 256, 384)
+
+        def prep_w0():
+            gw = wtmp.tile([P, 1152, 4], BF16, name="gw0", tag="gw", align_bytes=64)
+            for j in range(3):
+                regroup(gw[:, 384 * j : 384 * (j + 1), :], raw0[:, 4 * j : 4 * j + 4, :], False)
+            quant_w(w0c, w0s, gw, 0, 1024)
+            quant_w(w0c, w0s, gw, 1024, 1152)
+
+        def prep_w1_items():
+            items = []
+
+            def alloc():
+                wgrp["gw1"] = wtmp.tile([P, 1536, 4], BF16, name="gw1", tag="gw", align_bytes=64)
+
+            def rg(j, part):
+                def go():
+                    if "gw1" not in wgrp:
+                        alloc()
+                    gw = wgrp["gw1"]
+                    h = (1, 0, 1)[part]
+                    base = 768 * j + 256 * part
+                    regroup(gw[:, base : base + 256, :], raw1[:, (2 * h + j) * 4 : (2 * h + j) * 4 + 4, :], part == 2)
+
+                return go
+
+            def qq(lo, hi):
+                def go():
+                    quant_w(w1c, w1s, wgrp["gw1"], lo, hi)
+
+                return go
+
+            for j in range(2):
+                for part in range(3):
+                    items.append(rg(j, part))
+            items.append(qq(0, 1024))
+            items.append(qq(1024, 1536))
+            return items
+
+        moving = {}
+        for j in range(3):
+            moving[j] = (w0c, w0s, 384 * j)
+        for j in range(2):
+            moving[3 + j] = (w1c, w1s, 768 * j + 256)
+            moving[5 + j] = (w1c, w1s, 768 * j)
+        moving[7] = (w2c, w2s, 128)
+        moving[8] = (w2c, w2s, 0)
+        out_span = {"m0": (0, 384), "m1": (384, 512), "m2": (896, 256)}
+
+        opair = []
+        for j in range(NT // 2):
+            opair.append(outs.tile([P, 2, OUTW], F32, name="op%d" % j))
+
+        graw = {}
+        gcodes = {}
+
+        def load(s):
+            kind, c0, ncomp, t0, ntile = units[s]
+            g = ring.tile([P, ntile * ncomp * KP], BF16, name="graw", tag="graw")
+            nc.sync.dma_start(
+                out=g[:].rearrange("p (a k) -> p a k", a=ntile),
+                in_=gv[:, t0 : t0 + ntile, c0 * KP : (c0 + ncomp) * KP],
+            )
+            graw[s] = g
+
+        def transposes(s):
+            kind, c0, ncomp, t0, ntile = units[s]
+            nops = ntile * ncomp
+            words = graw[s][:].bitcast(F32)
+            grp = stage.tile([P, nops * KP], BF16, name="grp", tag="grp", align_bytes=64)
+            grpw = grp[:].bitcast(F32)
+            for b in range(nops // 2):
+                tb = psum.tile([P, 4, P], F32, name="tb", tag="tb")
+                for q in range(4):
+                    w_lo = (4 * b + q) * P
+                    nc.tensor.transpose(out=tb[:, q, :], in_=words[:, w_lo : w_lo + P], identity=ident[:])
+                nc.scalar.copy(
+                    out=grpw[:, b * 512 : (b + 1) * 512].rearrange("p (a e u) -> p a e u", a=2, u=2),
+                    in_=tb[:].rearrange("p (a u) e -> p a e u", u=2),
+                )
+            return grp
+
+        def quant_items(s, grp):
+            kind, c0, ncomp, t0, ntile = units[s]
+            nops = ntile * ncomp
+            gc = stage.tile([P, nops * P], U32, name="gc", tag="gc", align_bytes=64)
+            gs = stage.tile([P, nops * P], U8, name="gs", tag="gs", align_bytes=64)
+            gcodes[s] = (gc, gs)
+            items = []
+            lo = 0
+            total = nops * P
+            while lo < total:
+                width = 512
+                while lo + width > total:
+                    width //= 2
+
+                def go(lo=lo, hi=lo + width):
+                    nc.vector.quantize_mx(
+                        out=gc[:, lo:hi].bitcast(E5X4), scales=gs[:, lo:hi], in_=grp[:, 4 * lo : 4 * hi]
+                    )
+
+                items.append(go)
+                lo += width
+            return items
+
+        def passes(s):
+            kind, c0, ncomp, t0, ntile = units[s]
+            gc, gs = gcodes[s]
+            col0, width = out_span[kind]
+            items = []
+            for a in range(ntile):
+                ob = psum.tile([P, 512], F32, name="ob", tag="ob")
+                for ci in range(ncomp):
+                    o = a * ncomp + ci
+                    wc, ws, off = moving[c0 + ci]
+                    nc.tensor.matmul_mx(
+                        out=ob[:],
+                        lhsT=gc[:, o * P : (o + 1) * P].bitcast(E5X4),
+                        lhsT_scale=gs[:, o * P : (o + 1) * P],
+                        rhs=wc[:, off : off + 512].bitcast(E4X4),
+                        rhs_scale=ws[:, off : off + 512],
+                        start=(ci == 0),
+                        stop=(ci == ncomp - 1),
+                    )
+                t = t0 + a
+                on_scalar = kind == "m2" or (kind == "m0" and a == 1)
+
+                def go(ob=ob, t=t, on_scalar=on_scalar):
+                    dst = opair[t // 2][:, t % 2, col0 : col0 + width]
+                    if on_scalar:
+                        nc.scalar.copy(out=dst, in_=ob[:, 0:width])
+                    else:
+                        nc.vector.tensor_copy(out=dst, in_=ob[:, 0:width])
+                    if kind == "m1":
+                        if t >= NT - 2:
+                            nc.sync.dma_start(out=ov[:, t : t + 1, :], in_=opair[t // 2][:, t % 2 : t % 2 + 1, :])
+                        elif t % 2 == 1:
+                            nc.sync.dma_start(out=ov[:, t - 1 : t + 1, :], in_=opair[t // 2][:])
+
+                items.append(go)
+            return items
+
+        load_w(raw2, W2)
+        for s in range(6):
+            load(s)
+        load_w(raw0, W0)
+        load(6)
+        zero(w2c, w2s, 384, 640)
+        zero(w0c, w0s, 1152, 1280)
+        prep_w2()
+        w1_items = prep_w1_items()
+
+        for s in range(n + 1):
+            q_items = []
+            o_items = []
+            if s < n:
+                grp = transposes(s)
+                q_items = quant_items(s, grp)
+                if s + RING < n:
+                    load(s + RING)
+                if s == 3:
+                    load_w(raw1, W1)
+            if s >= 1:
+                o_items = passes(s - 1)
+            for i in range(max(len(q_items), len(o_items))):
+                if i < len(q_items):
+                    q_items[i]()
+                if i < len(o_items):
+                    o_items[i]()
+            if s == 5:
+                prep_w0()
+            if 9 <= s <= 12:
+                w1_items[2 * (s - 9)]()
+                w1_items[2 * (s - 9) + 1]()

@@ -15,7 +15,20 @@ KP = 512
 WPP = KP // 2
 CIN = 128
 OUTW = 9 * CIN
-RING = 7
+RING = 6
+NTB = 5
+NOB = 3
+CODE_BUFS = 5
+M2_SIZES = (1, 1, 2, 4, 4, 4)
+RUNS = (1, 1, 1, 1, 1, 1) + (2, 2, 2, 2) + (2, 2, 2, 2)
+DVE_EVERY = 3
+W2_LOAD_BEFORE = 0
+W0_LOAD_BEFORE = 6
+W1_LOAD_AFTER = 4
+W0_PREP_STEP = 5
+W1_PREP_STEPS = (6, 7, 8, 9)
+W1_PER_STEP = 2
+LATE = 12
 
 FLOPS = 2 * 2048 * (1536 * 384 + 4 * 1024 * 256 + 4 * 512 * 128)
 BYTES = 2048 * 9 * 512 * 2 + (1536 * 384 + 2048 * 256 + 1024 * 128) * 2 + 2048 * 9 * 128 * 4
@@ -26,7 +39,7 @@ PINNED = True
 def make_units():
     units = []
     t = 0
-    for size in (1, 1, 2, 4, 4, 4):
+    for size in M2_SIZES:
         units.append(("m2", 7, 2, t, size))
         t += size
     for t in range(0, NT, 2):
@@ -54,7 +67,7 @@ def body(tc, W0, W1, W2, grad_out, out):
     with tc.tile_pool(name="const", bufs=1) as const, tc.tile_pool(name="wtmp", bufs=1) as wtmp, tc.tile_pool(
         name="ring", bufs=RING
     ) as ring, tc.tile_pool(name="stage", bufs=3) as stage, tc.tile_pool(name="outs", bufs=1) as outs, tc.psum_pool(
-        name="psum", bufs=4
+        name="psum", bufs=1
     ) as psum:
         ident = const.tile([P, P], F32, name="ident")
         make_identity(nc, ident[:])
@@ -157,63 +170,64 @@ def body(tc, W0, W1, W2, grad_out, out):
 
         graw = {}
         gcodes = {}
+        counter = [0]
+        held = [None]
+        w1_next = [0]
 
-        def load(s):
-            kind, c0, ncomp, t0, ntile = units[s]
+        def load(gi):
+            kind, c0, ncomp, t0, ntile = units[gi]
             g = ring.tile([P, ntile * ncomp * KP], BF16, name="graw", tag="graw")
             nc.sync.dma_start(
                 out=g[:].rearrange("p (a k) -> p a k", a=ntile),
                 in_=gv[:, t0 : t0 + ntile, c0 * KP : (c0 + ncomp) * KP],
             )
-            graw[s] = g
+            graw[gi] = g
 
-        def transposes(s):
-            kind, c0, ncomp, t0, ntile = units[s]
+        def flush():
+            if held[0] is not None:
+                held[0]()
+            held[0] = None
+
+        def transposes(gi):
+            kind, c0, ncomp, t0, ntile = units[gi]
             nops = ntile * ncomp
-            words = graw[s][:].bitcast(F32)
+            words = graw[gi][:].bitcast(F32)
             grp = stage.tile([P, nops * KP], BF16, name="grp", tag="grp", align_bytes=64)
+            gc = stage.tile([P, nops * P], U32, name="gc", tag="gc", bufs=CODE_BUFS, align_bytes=64)
+            gs = stage.tile([P, nops * P], U8, name="gs", tag="gs", bufs=CODE_BUFS, align_bytes=64)
+            gcodes[gi] = (gc, gs)
             grpw = grp[:].bitcast(F32)
-            for b in range(nops // 2):
-                tb = psum.tile([P, 4, P], F32, name="tb", tag="tb")
+            nbanks = nops // 2
+            for b in range(nbanks):
+                tb = psum.tile([P, 4, P], F32, name="tb", tag="tb", bufs=NTB)
                 for q in range(4):
                     w_lo = (4 * b + q) * P
                     nc.tensor.transpose(out=tb[:, q, :], in_=words[:, w_lo : w_lo + P], identity=ident[:])
-                nc.scalar.copy(
-                    out=grpw[:, b * 512 : (b + 1) * 512].rearrange("p (a e u) -> p a e u", a=2, u=2),
-                    in_=tb[:].rearrange("p (a u) e -> p a e u", u=2),
-                )
-            return grp
+                dst = grpw[:, b * 512 : (b + 1) * 512].rearrange("p (a e u) -> p a e u", a=2, u=2)
+                src = tb[:].rearrange("p (a u) e -> p a e u", u=2)
+                counter[0] += 1
+                if counter[0] % DVE_EVERY == 0:
+                    nc.vector.tensor_copy(out=dst, in_=src)
+                else:
+                    nc.scalar.copy(out=dst, in_=src)
+                if b % 2 == 1 or b == nbanks - 1:
+                    lo = (b - b % 2) * 256
+                    hi = (b + 1) * 256
 
-        def quant_items(s, grp):
-            kind, c0, ncomp, t0, ntile = units[s]
-            nops = ntile * ncomp
-            gc = stage.tile([P, nops * P], U32, name="gc", tag="gc", align_bytes=64)
-            gs = stage.tile([P, nops * P], U8, name="gs", tag="gs", align_bytes=64)
-            gcodes[s] = (gc, gs)
-            items = []
-            lo = 0
-            total = nops * P
-            while lo < total:
-                width = 512
-                while lo + width > total:
-                    width //= 2
+                    def go(lo=lo, hi=hi, gc=gc, gs=gs, grp=grp):
+                        nc.vector.quantize_mx(
+                            out=gc[:, lo:hi].bitcast(E5X4), scales=gs[:, lo:hi], in_=grp[:, 4 * lo : 4 * hi]
+                        )
 
-                def go(lo=lo, hi=lo + width):
-                    nc.vector.quantize_mx(
-                        out=gc[:, lo:hi].bitcast(E5X4), scales=gs[:, lo:hi], in_=grp[:, 4 * lo : 4 * hi]
-                    )
+                    flush()
+                    held[0] = go
 
-                items.append(go)
-                lo += width
-            return items
-
-        def passes(s):
-            kind, c0, ncomp, t0, ntile = units[s]
-            gc, gs = gcodes[s]
+        def passes(gi):
+            kind, c0, ncomp, t0, ntile = units[gi]
+            gc, gs = gcodes[gi]
             col0, width = out_span[kind]
-            items = []
             for a in range(ntile):
-                ob = psum.tile([P, 512], F32, name="ob", tag="ob")
+                ob = psum.tile([P, 512], F32, name="ob", tag="ob", bufs=NOB)
                 for ci in range(ncomp):
                     o = a * ncomp + ci
                     wc, ws, off = moving[c0 + ci]
@@ -227,52 +241,52 @@ def body(tc, W0, W1, W2, grad_out, out):
                         stop=(ci == ncomp - 1),
                     )
                 t = t0 + a
-                on_scalar = kind == "m2" or (kind == "m0" and a == 1)
+                pair = opair[t // 2]
+                nc.scalar.copy(out=pair[:, t % 2, col0 : col0 + width], in_=ob[:, 0:width])
+                if kind == "m0" and t >= LATE and t % 2 == 1:
+                    nc.sync.dma_start(out=ov[:, t - 1 : t + 1, 0:384], in_=pair[:, :, 0:384])
+                    nc.sync.dma_start(out=ov[:, t - 1 : t + 1, 896:1152], in_=pair[:, :, 896:1152])
+                if kind == "m1":
+                    if t >= LATE:
+                        nc.sync.dma_start(out=ov[:, t : t + 1, 384:896], in_=pair[:, t % 2 : t % 2 + 1, 384:896])
+                    elif t % 2 == 1:
+                        nc.sync.dma_start(out=ov[:, t - 1 : t + 1, :], in_=pair[:])
 
-                def go(ob=ob, t=t, on_scalar=on_scalar):
-                    dst = opair[t // 2][:, t % 2, col0 : col0 + width]
-                    if on_scalar:
-                        nc.scalar.copy(out=dst, in_=ob[:, 0:width])
-                    else:
-                        nc.vector.tensor_copy(out=dst, in_=ob[:, 0:width])
-                    if kind == "m1":
-                        if t >= NT - 2:
-                            nc.sync.dma_start(out=ov[:, t : t + 1, :], in_=opair[t // 2][:, t % 2 : t % 2 + 1, :])
-                        elif t % 2 == 1:
-                            nc.sync.dma_start(out=ov[:, t - 1 : t + 1, :], in_=opair[t // 2][:])
-
-                items.append(go)
-            return items
-
-        load_w(raw2, W2)
-        for s in range(6):
-            load(s)
-        load_w(raw0, W0)
-        load(6)
+        for gi in range(RING):
+            if gi == W2_LOAD_BEFORE:
+                load_w(raw2, W2)
+            if gi == W0_LOAD_BEFORE:
+                load_w(raw0, W0)
+            load(gi)
+        if W0_LOAD_BEFORE >= RING:
+            load_w(raw0, W0)
         zero(w2c, w2s, 384, 640)
         zero(w0c, w0s, 1152, 1280)
         prep_w2()
         w1_items = prep_w1_items()
 
-        for s in range(n + 1):
-            q_items = []
-            o_items = []
-            if s < n:
-                grp = transposes(s)
-                q_items = quant_items(s, grp)
-                if s + RING < n:
-                    load(s + RING)
-                if s == 3:
-                    load_w(raw1, W1)
-            if s >= 1:
-                o_items = passes(s - 1)
-            for i in range(max(len(q_items), len(o_items))):
-                if i < len(q_items):
-                    q_items[i]()
-                if i < len(o_items):
-                    o_items[i]()
-            if s == 5:
+        runs = []
+        gi = 0
+        for size in RUNS:
+            runs.append(list(range(gi, gi + size)))
+            gi += size
+        assert gi == n
+
+        for s in range(len(runs) + 1):
+            if s < len(runs):
+                for gi in runs[s]:
+                    transposes(gi)
+                    if gi + RING < n:
+                        load(gi + RING)
+                    if gi == W1_LOAD_AFTER:
+                        load_w(raw1, W1)
+                flush()
+            if s == W0_PREP_STEP:
                 prep_w0()
-            if 9 <= s <= 12:
-                w1_items[2 * (s - 9)]()
-                w1_items[2 * (s - 9) + 1]()
+            if s in W1_PREP_STEPS:
+                for i in range(W1_PER_STEP):
+                    w1_items[w1_next[0]]()
+                    w1_next[0] += 1
+            if s >= 1:
+                for gi in runs[s - 1]:
+                    passes(gi)

@@ -20,14 +20,16 @@ NTB = 5
 NOB = 3
 CODE_BUFS = 5
 M2_SIZES = (1, 1, 2, 4, 4, 4)
-RUNS = (1, 1, 1, 1, 1, 1) + (2, 2, 2, 2) + (2, 2, 2, 2)
+RUNS = (1,) * 22
 DVE_EVERY = 3
 W2_LOAD_BEFORE = 0
 W0_LOAD_BEFORE = 6
 W1_LOAD_AFTER = 4
 W0_PREP_STEP = 5
-W1_PREP_STEPS = (6, 7, 8, 9)
+W1_PREP_STEPS = (9, 10, 11, 12)
 W1_PER_STEP = 2
+WARM = {-1: 6, 1: 2}
+SPANS = {"m0": ((0, 512),), "m1": ((0, 512),), "m2": ((0, 512),)}
 LATE = 12
 
 FLOPS = 2 * 2048 * (1536 * 384 + 4 * 1024 * 256 + 4 * 512 * 128)
@@ -71,6 +73,8 @@ def body(tc, W0, W1, W2, grad_out, out):
     ) as psum:
         ident = const.tile([P, P], F32, name="ident")
         make_identity(nc, ident[:])
+        zb = const.tile([P, 512], BF16, name="zb")
+        nc.vector.memset(zb[:], 0.0)
 
         w0c = const.tile([P, 1280], U32, name="w0c", align_bytes=64)
         w0s = const.tile([P, 1280], U8, name="w0s", align_bytes=64)
@@ -228,18 +232,19 @@ def body(tc, W0, W1, W2, grad_out, out):
             col0, width = out_span[kind]
             for a in range(ntile):
                 ob = psum.tile([P, 512], F32, name="ob", tag="ob", bufs=NOB)
-                for ci in range(ncomp):
-                    o = a * ncomp + ci
-                    wc, ws, off = moving[c0 + ci]
-                    nc.tensor.matmul_mx(
-                        out=ob[:],
-                        lhsT=gc[:, o * P : (o + 1) * P].bitcast(E5X4),
-                        lhsT_scale=gs[:, o * P : (o + 1) * P],
-                        rhs=wc[:, off : off + 512].bitcast(E4X4),
-                        rhs_scale=ws[:, off : off + 512],
-                        start=(ci == 0),
-                        stop=(ci == ncomp - 1),
-                    )
+                for lo, hi in SPANS[kind]:
+                    for ci in range(ncomp):
+                        o = a * ncomp + ci
+                        wc, ws, off = moving[c0 + ci]
+                        nc.tensor.matmul_mx(
+                            out=ob[:, lo:hi],
+                            lhsT=gc[:, o * P : (o + 1) * P].bitcast(E5X4),
+                            lhsT_scale=gs[:, o * P : (o + 1) * P],
+                            rhs=wc[:, off + lo : off + hi].bitcast(E4X4),
+                            rhs_scale=ws[:, off + lo : off + hi],
+                            start=(ci == 0),
+                            stop=(ci == ncomp - 1),
+                        )
                 t = t0 + a
                 pair = opair[t // 2]
                 nc.scalar.copy(out=pair[:, t % 2, col0 : col0 + width], in_=ob[:, 0:width])
@@ -265,6 +270,12 @@ def body(tc, W0, W1, W2, grad_out, out):
         prep_w2()
         w1_items = prep_w1_items()
 
+        def warm(count):
+            for i in range(count):
+                wb = psum.tile([P, 512], F32, name="wb", tag="ob", bufs=NOB)
+                nc.tensor.matmul(out=wb[:], lhsT=zb[:, 0:P], rhs=zb[:], start=True, stop=True)
+
+        warm(WARM.get(-1, 0))
         runs = []
         gi = 0
         for size in RUNS:
@@ -281,6 +292,7 @@ def body(tc, W0, W1, W2, grad_out, out):
                     if gi == W1_LOAD_AFTER:
                         load_w(raw1, W1)
                 flush()
+            warm(WARM.get(s, 0))
             if s == W0_PREP_STEP:
                 prep_w0()
             if s in W1_PREP_STEPS:

@@ -12,30 +12,26 @@ E5X4 = mybir.dt.float8_e5m2_x4
 P = 128
 NT = 16
 KP = 512
-WPP = KP // 2
 CIN = 128
 OUTW = 9 * CIN
 RING = 6
 NTB = 5
 NOB = 3
+GRP_BUFS = 3
 CODE_BUFS = 5
 M2_SIZES = (1, 1, 2, 4, 4, 4)
-RUNS = (1,) * 22
-DVE_EVERY = 3
-W2_LOAD_BEFORE = 0
-W0_LOAD_BEFORE = 6
-W1_LOAD_AFTER = 4
-W0_PREP_STEP = 5
-W1_PREP_STEPS = (9, 10, 11, 12)
-W1_PER_STEP = 2
+CYCLES = (1, 1, 1, 1, 1, 1, 2, 2, 2, 2, 2, 2, 2, 2)
+EVAC = {"m2": "SSSV", "m0": "SSSV", "m1": "VS"}
+W2_LOAD_AFTER = -1
+W0_LOAD_AFTER = 5
+W1_LOAD_AFTER = 10
+W0_PREP = {4: 1, 5: 2, 6: 2}
+W1_PREP = {6: 2, 7: 2, 8: 2, 9: 2}
 WARM = {-1: 6, 1: 2}
-SPANS = {"m0": ((0, 512),), "m1": ((0, 512),), "m2": ((0, 512),)}
 LATE = 12
 
 FLOPS = 2 * 2048 * (1536 * 384 + 4 * 1024 * 256 + 4 * 512 * 128)
 BYTES = 2048 * 9 * 512 * 2 + (1536 * 384 + 2048 * 256 + 1024 * 128) * 2 + 2048 * 9 * 128 * 4
-
-PINNED = True
 
 
 def make_units():
@@ -52,10 +48,7 @@ def make_units():
 
 
 def tile_so2linear_t_kernel(tc, x, W0, b0, W1, W2, grad_out, out):
-    if PINNED:
-        with tc.manual_schedule():
-            body(tc, W0, W1, W2, grad_out, out)
-    else:
+    with tc.manual_schedule():
         body(tc, W0, W1, W2, grad_out, out)
 
 
@@ -68,7 +61,7 @@ def body(tc, W0, W1, W2, grad_out, out):
 
     with tc.tile_pool(name="const", bufs=1) as const, tc.tile_pool(name="wtmp", bufs=1) as wtmp, tc.tile_pool(
         name="ring", bufs=RING
-    ) as ring, tc.tile_pool(name="stage", bufs=3) as stage, tc.tile_pool(name="outs", bufs=1) as outs, tc.psum_pool(
+    ) as ring, tc.tile_pool(name="stage", bufs=GRP_BUFS) as stage, tc.tile_pool(name="outs", bufs=1) as outs, tc.psum_pool(
         name="psum", bufs=1
     ) as psum:
         ident = const.tile([P, P], F32, name="ident")
@@ -85,6 +78,12 @@ def body(tc, W0, W1, W2, grad_out, out):
         raw0 = wtmp.tile([P, 12, 384], BF16, name="raw0")
         raw1 = wtmp.tile([P, 16, 256], BF16, name="raw1")
         raw2 = wtmp.tile([P, 8, 128], BF16, name="raw2")
+        grouped = {}
+
+        def grouped_tile(which, width):
+            if which not in grouped:
+                grouped[which] = wtmp.tile([P, width, 4], BF16, name="gw%d" % which, tag="gw", align_bytes=64)
+            return grouped[which]
 
         def load_w(raw, w):
             nc.sync.dma_start(
@@ -92,71 +91,56 @@ def body(tc, W0, W1, W2, grad_out, out):
                 in_=w.rearrange("(a p e) c -> p a (e c)", p=P, e=2),
             )
 
-        def regroup(dst, src, negate):
+        def regroup(dst, src):
             d = dst.rearrange("p (c i) t -> p c t i", i=4)
             s = src.rearrange("p t (c i) -> p c t i", i=4)
-            if negate:
-                nc.vector.tensor_scalar_mul(out=d, in0=s, scalar1=-1.0)
-            else:
-                nc.vector.tensor_copy(out=d, in_=s)
+            nc.vector.tensor_copy(out=d, in_=s)
 
-        def quant_w(codes, scales, grouped, lo, hi):
+        def negate(gw, dst, src, width):
+            nc.vector.tensor_scalar_mul(
+                out=gw[:, dst : dst + width, :].rearrange("p c t -> p (c t)"),
+                in0=gw[:, src : src + width, :].rearrange("p c t -> p (c t)"),
+                scalar1=-1.0,
+            )
+
+        def quant_w(codes, scales, gw, lo, hi):
             nc.vector.quantize_mx(
                 out=codes[:, lo:hi].bitcast(E4X4),
                 scales=scales[:, lo:hi],
-                in_=grouped[:, lo:hi, :].rearrange("p c t -> p (c t)"),
+                in_=gw[:, lo:hi, :].rearrange("p c t -> p (c t)"),
             )
 
         def zero(codes, scales, lo, hi):
             nc.vector.memset(codes[:, lo:hi].bitcast(I32), 0)
             nc.vector.memset(scales[:, lo:hi].bitcast(I32), 0)
 
-        wgrp = {}
-
         def prep_w2():
-            gw = wtmp.tile([P, 384, 4], BF16, name="gw2", tag="gw", align_bytes=64)
-            regroup(gw[:, 0:128, :], raw2[:, 4:8, :], False)
-            regroup(gw[:, 128:256, :], raw2[:, 0:4, :], False)
-            regroup(gw[:, 256:384, :], raw2[:, 4:8, :], True)
-            quant_w(w2c, w2s, gw, 0, 256)
-            quant_w(w2c, w2s, gw, 256, 384)
+            gw2 = grouped_tile(2, 384)
+            regroup(gw2[:, 0:128, :], raw2[:, 4:8, :])
+            regroup(gw2[:, 128:256, :], raw2[:, 0:4, :])
+            negate(gw2, 256, 0, 128)
+            quant_w(w2c, w2s, gw2, 0, 256)
+            quant_w(w2c, w2s, gw2, 256, 384)
 
-        def prep_w0():
-            gw = wtmp.tile([P, 1152, 4], BF16, name="gw0", tag="gw", align_bytes=64)
-            for j in range(3):
-                regroup(gw[:, 384 * j : 384 * (j + 1), :], raw0[:, 4 * j : 4 * j + 4, :], False)
-            quant_w(w0c, w0s, gw, 0, 1024)
-            quant_w(w0c, w0s, gw, 1024, 1152)
+        w0_items = []
+        for j in range(3):
+            w0_items.append(lambda j=j: regroup(grouped_tile(0, 1152)[:, 384 * j : 384 * (j + 1), :], raw0[:, 4 * j : 4 * j + 4, :]))
+        w0_items.append(lambda: quant_w(w0c, w0s, grouped_tile(0, 1152), 0, 1024))
+        w0_items.append(lambda: quant_w(w0c, w0s, grouped_tile(0, 1152), 1024, 1152))
 
-        def prep_w1_items():
-            items = []
-
-            def alloc():
-                wgrp["gw1"] = wtmp.tile([P, 1536, 4], BF16, name="gw1", tag="gw", align_bytes=64)
-
-            def rg(j, part):
-                def go():
-                    if "gw1" not in wgrp:
-                        alloc()
-                    gw = wgrp["gw1"]
-                    h = (1, 0, 1)[part]
-                    base = 768 * j + 256 * part
-                    regroup(gw[:, base : base + 256, :], raw1[:, (2 * h + j) * 4 : (2 * h + j) * 4 + 4, :], part == 2)
-
-                return go
-
-            def qq(lo, hi):
-                def go():
-                    quant_w(w1c, w1s, wgrp["gw1"], lo, hi)
-
-                return go
-
-            for j in range(2):
-                for part in range(3):
-                    items.append(rg(j, part))
-            items.append(qq(0, 1024))
-            items.append(qq(1024, 1536))
-            return items
+        w1_items = []
+        for j in range(2):
+            for part in range(2):
+                h = 1 - part
+                base = 768 * j + 256 * part
+                w1_items.append(
+                    lambda j=j, h=h, base=base: regroup(
+                        grouped_tile(1, 1536)[:, base : base + 256, :], raw1[:, (2 * h + j) * 4 : (2 * h + j) * 4 + 4, :]
+                    )
+                )
+            w1_items.append(lambda j=j: negate(grouped_tile(1, 1536), 768 * j + 512, 768 * j, 256))
+        w1_items.append(lambda: quant_w(w1c, w1s, grouped_tile(1, 1536), 0, 1024))
+        w1_items.append(lambda: quant_w(w1c, w1s, grouped_tile(1, 1536), 1024, 1536))
 
         moving = {}
         for j in range(3):
@@ -174,9 +158,9 @@ def body(tc, W0, W1, W2, grad_out, out):
 
         graw = {}
         gcodes = {}
-        counter = [0]
-        held = [None]
+        w0_next = [0]
         w1_next = [0]
+        waiting = []
 
         def load(gi):
             kind, c0, ncomp, t0, ntile = units[gi]
@@ -186,13 +170,12 @@ def body(tc, W0, W1, W2, grad_out, out):
                 in_=gv[:, t0 : t0 + ntile, c0 * KP : (c0 + ncomp) * KP],
             )
             graw[gi] = g
+            if gi == W0_LOAD_AFTER:
+                load_w(raw0, W0)
+            if gi == W1_LOAD_AFTER:
+                load_w(raw1, W1)
 
-        def flush():
-            if held[0] is not None:
-                held[0]()
-            held[0] = None
-
-        def transposes(gi):
+        def transposes(gi, turn):
             kind, c0, ncomp, t0, ntile = units[gi]
             nops = ntile * ncomp
             words = graw[gi][:].bitcast(F32)
@@ -202,6 +185,7 @@ def body(tc, W0, W1, W2, grad_out, out):
             gcodes[gi] = (gc, gs)
             grpw = grp[:].bitcast(F32)
             nbanks = nops // 2
+            who = EVAC[kind]
             for b in range(nbanks):
                 tb = psum.tile([P, 4, P], F32, name="tb", tag="tb", bufs=NTB)
                 for q in range(4):
@@ -209,22 +193,20 @@ def body(tc, W0, W1, W2, grad_out, out):
                     nc.tensor.transpose(out=tb[:, q, :], in_=words[:, w_lo : w_lo + P], identity=ident[:])
                 dst = grpw[:, b * 512 : (b + 1) * 512].rearrange("p (a e u) -> p a e u", a=2, u=2)
                 src = tb[:].rearrange("p (a u) e -> p a e u", u=2)
-                counter[0] += 1
-                if counter[0] % DVE_EVERY == 0:
+                if who[turn % len(who)] == "V":
                     nc.vector.tensor_copy(out=dst, in_=src)
                 else:
                     nc.scalar.copy(out=dst, in_=src)
+                turn += 1
                 if b % 2 == 1 or b == nbanks - 1:
                     lo = (b - b % 2) * 256
                     hi = (b + 1) * 256
-
-                    def go(lo=lo, hi=hi, gc=gc, gs=gs, grp=grp):
-                        nc.vector.quantize_mx(
+                    waiting.append(
+                        lambda lo=lo, hi=hi, gc=gc, gs=gs, grp=grp: nc.vector.quantize_mx(
                             out=gc[:, lo:hi].bitcast(E5X4), scales=gs[:, lo:hi], in_=grp[:, 4 * lo : 4 * hi]
                         )
-
-                    flush()
-                    held[0] = go
+                    )
+            return turn
 
         def passes(gi):
             kind, c0, ncomp, t0, ntile = units[gi]
@@ -232,19 +214,18 @@ def body(tc, W0, W1, W2, grad_out, out):
             col0, width = out_span[kind]
             for a in range(ntile):
                 ob = psum.tile([P, 512], F32, name="ob", tag="ob", bufs=NOB)
-                for lo, hi in SPANS[kind]:
-                    for ci in range(ncomp):
-                        o = a * ncomp + ci
-                        wc, ws, off = moving[c0 + ci]
-                        nc.tensor.matmul_mx(
-                            out=ob[:, lo:hi],
-                            lhsT=gc[:, o * P : (o + 1) * P].bitcast(E5X4),
-                            lhsT_scale=gs[:, o * P : (o + 1) * P],
-                            rhs=wc[:, off + lo : off + hi].bitcast(E4X4),
-                            rhs_scale=ws[:, off + lo : off + hi],
-                            start=(ci == 0),
-                            stop=(ci == ncomp - 1),
-                        )
+                for ci in range(ncomp):
+                    o = a * ncomp + ci
+                    wc, ws, off = moving[c0 + ci]
+                    nc.tensor.matmul_mx(
+                        out=ob[:],
+                        lhsT=gc[:, o * P : (o + 1) * P].bitcast(E5X4),
+                        lhsT_scale=gs[:, o * P : (o + 1) * P],
+                        rhs=wc[:, off : off + 512].bitcast(E4X4),
+                        rhs_scale=ws[:, off : off + 512],
+                        start=(ci == 0),
+                        stop=(ci == ncomp - 1),
+                    )
                 t = t0 + a
                 pair = opair[t // 2]
                 nc.scalar.copy(out=pair[:, t % 2, col0 : col0 + width], in_=ob[:, 0:width])
@@ -257,48 +238,46 @@ def body(tc, W0, W1, W2, grad_out, out):
                     elif t % 2 == 1:
                         nc.sync.dma_start(out=ov[:, t - 1 : t + 1, :], in_=pair[:])
 
-        for gi in range(RING):
-            if gi == W2_LOAD_BEFORE:
-                load_w(raw2, W2)
-            if gi == W0_LOAD_BEFORE:
-                load_w(raw0, W0)
-            load(gi)
-        if W0_LOAD_BEFORE >= RING:
-            load_w(raw0, W0)
-        zero(w2c, w2s, 384, 640)
-        zero(w0c, w0s, 1152, 1280)
-        prep_w2()
-        w1_items = prep_w1_items()
-
         def warm(count):
             for i in range(count):
                 wb = psum.tile([P, 512], F32, name="wb", tag="ob", bufs=NOB)
                 nc.tensor.matmul(out=wb[:], lhsT=zb[:, 0:P], rhs=zb[:], start=True, stop=True)
 
+        if W2_LOAD_AFTER < 0:
+            load_w(raw2, W2)
+        for gi in range(RING):
+            load(gi)
+            if gi == W2_LOAD_AFTER:
+                load_w(raw2, W2)
+        zero(w2c, w2s, 384, 640)
+        zero(w0c, w0s, 1152, 1280)
+        prep_w2()
         warm(WARM.get(-1, 0))
-        runs = []
+
+        cycles = []
         gi = 0
-        for size in RUNS:
-            runs.append(list(range(gi, gi + size)))
+        for size in CYCLES:
+            cycles.append(list(range(gi, gi + size)))
             gi += size
         assert gi == n
 
-        for s in range(len(runs) + 1):
-            if s < len(runs):
-                for gi in runs[s]:
-                    transposes(gi)
+        for s in range(len(cycles) + 1):
+            if s < len(cycles):
+                turn = 0
+                for gi in cycles[s]:
+                    turn = transposes(gi, turn)
                     if gi + RING < n:
                         load(gi + RING)
-                    if gi == W1_LOAD_AFTER:
-                        load_w(raw1, W1)
-                flush()
             warm(WARM.get(s, 0))
-            if s == W0_PREP_STEP:
-                prep_w0()
-            if s in W1_PREP_STEPS:
-                for i in range(W1_PER_STEP):
-                    w1_items[w1_next[0]]()
-                    w1_next[0] += 1
             if s >= 1:
-                for gi in runs[s - 1]:
+                for gi in cycles[s - 1]:
                     passes(gi)
+            for go in waiting:
+                go()
+            waiting.clear()
+            for i in range(W0_PREP.get(s, 0)):
+                w0_items[w0_next[0]]()
+                w0_next[0] += 1
+            for i in range(W1_PREP.get(s, 0)):
+                w1_items[w1_next[0]]()
+                w1_next[0] += 1

@@ -20,13 +20,14 @@ NOB = 3
 GRP_BUFS = 3
 CODE_BUFS = 5
 M2_SIZES = (1, 1, 2, 4, 4, 4)
-CYCLES = (1, 1, 1, 1, 1, 1, 2, 2, 2, 2, 2, 2, 2, 2)
+PIECE = {"m2": 2, "m0": 2, "m1": 1}
+LAG = 2
 EVAC = {"m2": "SSSV", "m0": "SSSV", "m1": "VS"}
 W2_LOAD_AFTER = -1
 W0_LOAD_AFTER = 5
 W1_LOAD_AFTER = 10
 W0_PREP = {4: 1, 5: 2, 6: 2}
-W1_PREP = {6: 2, 7: 2, 8: 2, 9: 2}
+W1_PREP = {9: 1, 10: 2, 11: 2, 12: 2, 13: 1}
 WARM = {-1: 6, 1: 2}
 LATE = 12
 
@@ -175,16 +176,17 @@ def body(tc, W0, W1, W2, grad_out, out):
             if gi == W1_LOAD_AFTER:
                 load_w(raw1, W1)
 
-        def transposes(gi, turn):
-            kind, c0, ncomp, t0, ntile = units[gi]
+        def transposes(piece, turn):
+            gi, a0, ntile = piece
+            kind, c0, ncomp, t0, unit_tiles = units[gi]
             nops = ntile * ncomp
-            words = graw[gi][:].bitcast(F32)
+            words = graw[gi][:, a0 * ncomp * KP : (a0 + ntile) * ncomp * KP].bitcast(F32)
             grp = stage.tile([P, nops * KP], BF16, name="grp", tag="grp", align_bytes=64)
             gc = stage.tile([P, nops * P], U32, name="gc", tag="gc", bufs=CODE_BUFS, align_bytes=64)
             gs = stage.tile([P, nops * P], U8, name="gs", tag="gs", bufs=CODE_BUFS, align_bytes=64)
-            gcodes[gi] = (gc, gs)
+            gcodes[piece] = (gc, gs)
             grpw = grp[:].bitcast(F32)
-            nbanks = nops // 2
+            nbanks = (nops + 1) // 2
             who = EVAC[kind]
             for b in range(nbanks):
                 tb = psum.tile([P, 4, P], F32, name="tb", tag="tb", bufs=NTB)
@@ -208,9 +210,11 @@ def body(tc, W0, W1, W2, grad_out, out):
                     )
             return turn
 
-        def passes(gi):
-            kind, c0, ncomp, t0, ntile = units[gi]
-            gc, gs = gcodes[gi]
+        def passes(piece):
+            gi, a0, ntile = piece
+            kind, c0, ncomp, t0, unit_tiles = units[gi]
+            t0 = t0 + a0
+            gc, gs = gcodes[piece]
             col0, width = out_span[kind]
             for a in range(ntile):
                 ob = psum.tile([P, 512], F32, name="ob", tag="ob", bufs=NOB)
@@ -254,30 +258,30 @@ def body(tc, W0, W1, W2, grad_out, out):
         prep_w2()
         warm(WARM.get(-1, 0))
 
-        cycles = []
-        gi = 0
-        for size in CYCLES:
-            cycles.append(list(range(gi, gi + size)))
-            gi += size
-        assert gi == n
+        pieces = []
+        for gi in range(n):
+            kind, c0, ncomp, t0, ntile = units[gi]
+            step = min(PIECE[kind], ntile)
+            for a0 in range(0, ntile, step):
+                pieces.append((gi, a0, step))
 
-        for s in range(len(cycles) + 1):
-            if s < len(cycles):
-                turn = 0
-                for gi in cycles[s]:
-                    turn = transposes(gi, turn)
-                    if gi + RING < n:
-                        load(gi + RING)
+        for s in range(len(pieces) + LAG):
+            if s < len(pieces):
+                gi, a0, ntile = pieces[s]
+                transposes(pieces[s], s)
+                last = a0 + ntile == units[gi][4]
+                if last and gi + RING < n:
+                    load(gi + RING)
             warm(WARM.get(s, 0))
-            if s >= 1:
-                for gi in cycles[s - 1]:
-                    passes(gi)
+            if s >= LAG:
+                passes(pieces[s - LAG])
             for go in waiting:
                 go()
             waiting.clear()
-            for i in range(W0_PREP.get(s, 0)):
-                w0_items[w0_next[0]]()
-                w0_next[0] += 1
-            for i in range(W1_PREP.get(s, 0)):
-                w1_items[w1_next[0]]()
-                w1_next[0] += 1
+            if s < len(pieces) and last:
+                for i in range(W0_PREP.get(gi, 0)):
+                    w0_items[w0_next[0]]()
+                    w0_next[0] += 1
+                for i in range(W1_PREP.get(gi, 0)):
+                    w1_items[w1_next[0]]()
+                    w1_next[0] += 1

@@ -14,20 +14,20 @@ NT = 16
 KP = 512
 CIN = 128
 OUTW = 9 * CIN
-RING = 6
+RING = 7
 NTB = 5
 NOB = 3
 GRP_BUFS = 3
 CODE_BUFS = 5
-M2_SIZES = (1, 1, 2, 4, 4, 4)
-PIECE = {"m2": 2, "m0": 2, "m1": 1}
+M2_SIZES = (1, 1, 2, 2, 2, 4, 4)
+PIECES = {"m2": (2, 2) + (4,) * 7, "m0": (6,) * 8, "m1": (4,) * 16}
 LAG = 2
 EVAC = {"m2": "SSSV", "m0": "SSSV", "m1": "VS"}
 W2_LOAD_AFTER = -1
-W0_LOAD_AFTER = 5
-W1_LOAD_AFTER = 10
-W0_PREP = {4: 1, 5: 2, 6: 2}
-W1_PREP = {9: 1, 10: 2, 11: 2, 12: 2, 13: 1}
+W0_LOAD_AFTER = 6
+W1_LOAD_AFTER = 11
+W0_PREP = {5: 1, 6: 2, 7: 2}
+W1_PREP = {10: 1, 11: 2, 12: 2, 13: 2, 14: 1}
 WARM = {-1: 6, 1: 2}
 LATE = 12
 
@@ -161,6 +161,7 @@ def body(tc, W0, W1, W2, grad_out, out):
         gcodes = {}
         w0_next = [0]
         w1_next = [0]
+        group = [None]
         waiting = []
 
         def load(gi):
@@ -177,29 +178,29 @@ def body(tc, W0, W1, W2, grad_out, out):
                 load_w(raw1, W1)
 
         def transposes(piece, turn):
-            gi, a0, ntile = piece
-            kind, c0, ncomp, t0, unit_tiles = units[gi]
-            nops = ntile * ncomp
-            words = graw[gi][:, a0 * ncomp * KP : (a0 + ntile) * ncomp * KP].bitcast(F32)
+            nops = len(piece)
+            kind = units[piece[0][0]][0]
             grp = stage.tile([P, nops * KP], BF16, name="grp", tag="grp", align_bytes=64)
             gc = stage.tile([P, nops * P], U32, name="gc", tag="gc", bufs=CODE_BUFS, align_bytes=64)
             gs = stage.tile([P, nops * P], U8, name="gs", tag="gs", bufs=CODE_BUFS, align_bytes=64)
-            gcodes[piece] = (gc, gs)
+            gcodes[piece[0]] = (gc, gs)
             grpw = grp[:].bitcast(F32)
-            nbanks = (nops + 1) // 2
+            nbanks = nops // 2
             who = EVAC[kind]
+            done = []
             for b in range(nbanks):
+                gi, o = piece[2 * b]
+                words = graw[gi][:].bitcast(F32)
                 tb = psum.tile([P, 4, P], F32, name="tb", tag="tb", bufs=NTB)
                 for q in range(4):
-                    w_lo = (4 * b + q) * P
+                    w_lo = (2 * o + q) * P
                     nc.tensor.transpose(out=tb[:, q, :], in_=words[:, w_lo : w_lo + P], identity=ident[:])
                 dst = grpw[:, b * 512 : (b + 1) * 512].rearrange("p (a e u) -> p a e u", a=2, u=2)
                 src = tb[:].rearrange("p (a u) e -> p a e u", u=2)
-                if who[turn % len(who)] == "V":
+                if who[(turn + b) % len(who)] == "V":
                     nc.vector.tensor_copy(out=dst, in_=src)
                 else:
                     nc.scalar.copy(out=dst, in_=src)
-                turn += 1
                 if b % 2 == 1 or b == nbanks - 1:
                     lo = (b - b % 2) * 256
                     hi = (b + 1) * 256
@@ -208,39 +209,47 @@ def body(tc, W0, W1, W2, grad_out, out):
                             out=gc[:, lo:hi].bitcast(E5X4), scales=gs[:, lo:hi], in_=grp[:, 4 * lo : 4 * hi]
                         )
                     )
-            return turn
+                if o + 2 == units[gi][2] * units[gi][4]:
+                    done.append(gi)
+                    if gi + RING < n:
+                        load(gi + RING)
+            return done
+
+        def finish(kind, t, ob):
+            col0, width = out_span[kind]
+            pair = opair[t // 2]
+            nc.scalar.copy(out=pair[:, t % 2, col0 : col0 + width], in_=ob[:, 0:width])
+            if kind == "m0" and t >= LATE and t % 2 == 1:
+                nc.sync.dma_start(out=ov[:, t - 1 : t + 1, 0:384], in_=pair[:, :, 0:384])
+                nc.sync.dma_start(out=ov[:, t - 1 : t + 1, 896:1152], in_=pair[:, :, 896:1152])
+            if kind == "m1":
+                if t >= LATE:
+                    nc.sync.dma_start(out=ov[:, t : t + 1, 384:896], in_=pair[:, t % 2 : t % 2 + 1, 384:896])
+                elif t % 2 == 1:
+                    nc.sync.dma_start(out=ov[:, t - 1 : t + 1, :], in_=pair[:])
 
         def passes(piece):
-            gi, a0, ntile = piece
-            kind, c0, ncomp, t0, unit_tiles = units[gi]
-            t0 = t0 + a0
-            gc, gs = gcodes[piece]
-            col0, width = out_span[kind]
-            for a in range(ntile):
-                ob = psum.tile([P, 512], F32, name="ob", tag="ob", bufs=NOB)
-                for ci in range(ncomp):
-                    o = a * ncomp + ci
-                    wc, ws, off = moving[c0 + ci]
-                    nc.tensor.matmul_mx(
-                        out=ob[:],
-                        lhsT=gc[:, o * P : (o + 1) * P].bitcast(E5X4),
-                        lhsT_scale=gs[:, o * P : (o + 1) * P],
-                        rhs=wc[:, off : off + 512].bitcast(E4X4),
-                        rhs_scale=ws[:, off : off + 512],
-                        start=(ci == 0),
-                        stop=(ci == ncomp - 1),
-                    )
-                t = t0 + a
-                pair = opair[t // 2]
-                nc.scalar.copy(out=pair[:, t % 2, col0 : col0 + width], in_=ob[:, 0:width])
-                if kind == "m0" and t >= LATE and t % 2 == 1:
-                    nc.sync.dma_start(out=ov[:, t - 1 : t + 1, 0:384], in_=pair[:, :, 0:384])
-                    nc.sync.dma_start(out=ov[:, t - 1 : t + 1, 896:1152], in_=pair[:, :, 896:1152])
-                if kind == "m1":
-                    if t >= LATE:
-                        nc.sync.dma_start(out=ov[:, t : t + 1, 384:896], in_=pair[:, t % 2 : t % 2 + 1, 384:896])
-                    elif t % 2 == 1:
-                        nc.sync.dma_start(out=ov[:, t - 1 : t + 1, :], in_=pair[:])
+            gc, gs = gcodes[piece[0]]
+            for i in range(len(piece)):
+                gi, o = piece[i]
+                kind, c0, ncomp, t0, ntile = units[gi]
+                a = o // ncomp
+                ci = o % ncomp
+                if ci == 0:
+                    group[0] = psum.tile([P, 512], F32, name="ob", tag="ob", bufs=NOB)
+                ob = group[0]
+                wc, ws, off = moving[c0 + ci]
+                nc.tensor.matmul_mx(
+                    out=ob[:],
+                    lhsT=gc[:, i * P : (i + 1) * P].bitcast(E5X4),
+                    lhsT_scale=gs[:, i * P : (i + 1) * P],
+                    rhs=wc[:, off : off + 512].bitcast(E4X4),
+                    rhs_scale=ws[:, off : off + 512],
+                    start=(ci == 0),
+                    stop=(ci == ncomp - 1),
+                )
+                if ci == ncomp - 1:
+                    finish(kind, t0 + a, ob)
 
         def warm(count):
             for i in range(count):
@@ -259,26 +268,29 @@ def body(tc, W0, W1, W2, grad_out, out):
         warm(WARM.get(-1, 0))
 
         pieces = []
-        for gi in range(n):
-            kind, c0, ncomp, t0, ntile = units[gi]
-            step = min(PIECE[kind], ntile)
-            for a0 in range(0, ntile, step):
-                pieces.append((gi, a0, step))
+        for kind in ("m2", "m0", "m1"):
+            stream = []
+            for gi in range(n):
+                if units[gi][0] == kind:
+                    for o in range(units[gi][2] * units[gi][4]):
+                        stream.append((gi, o))
+            lo = 0
+            for size in PIECES[kind]:
+                pieces.append(tuple(stream[lo : lo + size]))
+                lo += size
+            assert lo == len(stream)
 
         for s in range(len(pieces) + LAG):
+            done = []
             if s < len(pieces):
-                gi, a0, ntile = pieces[s]
-                transposes(pieces[s], s)
-                last = a0 + ntile == units[gi][4]
-                if last and gi + RING < n:
-                    load(gi + RING)
+                done = transposes(pieces[s], s)
             warm(WARM.get(s, 0))
             if s >= LAG:
                 passes(pieces[s - LAG])
             for go in waiting:
                 go()
             waiting.clear()
-            if s < len(pieces) and last:
+            for gi in done:
                 for i in range(W0_PREP.get(gi, 0)):
                     w0_items[w0_next[0]]()
                     w0_next[0] += 1

import concourse.mybir as mybir
from concourse.masks import make_identity

F32 = mybir.dt.float32
BF16 = mybir.dt.bfloat16
U32 = mybir.dt.uint32
U8 = mybir.dt.uint8
I32 = mybir.dt.int32
E4X4 = mybir.dt.float8_e4m3fn_x4
E5X4 = mybir.dt.float8_e5m2_x4

P = 128
NT = 16
KP = 512
CIN = 128
OUTW = 9 * CIN
RING = 7
NTB = 5
NOB = 3
GRP_BUFS = 3
CODE_BUFS = 5
M2_SIZES = (1, 1, 2, 2, 2, 4, 4)
PIECES = {"m2": (2, 2) + (4,) * 7, "m0": (6,) * 8, "m1": (4,) * 16}
LAG = 2
EVAC = {"m2": "SSSV", "m0": "SSSV", "m1": "VS"}
W2_LOAD_AFTER = -1
W0_LOAD_AFTER = 6
W1_LOAD_AFTER = 11
W0_PREP = {5: 1, 6: 2, 7: 2}
W1_PREP = {10: 1, 11: 2, 12: 2, 13: 2, 14: 1}
WARM = {-1: 6, 1: 2}
LATE = 12

FLOPS = 2 * 2048 * (1536 * 384 + 4 * 1024 * 256 + 4 * 512 * 128)
BYTES = 2048 * 9 * 512 * 2 + (1536 * 384 + 2048 * 256 + 1024 * 128) * 2 + 2048 * 9 * 128 * 4


def make_units():
    units = []
    t = 0
    for size in M2_SIZES:
        units.append(("m2", 7, 2, t, size))
        t += size
    for t in range(0, NT, 2):
        units.append(("m0", 0, 3, t, 2))
    for t in range(0, NT, 2):
        units.append(("m1", 3, 4, t, 2))
    return units


def tile_so2linear_t_kernel(tc, x, W0, b0, W1, W2, grad_out, out):
    with tc.manual_schedule():
        body(tc, W0, W1, W2, grad_out, out)


def body(tc, W0, W1, W2, grad_out, out):
    nc = tc.nc
    gv = grad_out.rearrange("(p t) c k -> p t (c k)", t=NT)
    ov = out.rearrange("(p t) c k -> p t (c k)", t=NT)
    units = make_units()
    n = len(units)

    with tc.tile_pool(name="const", bufs=1) as const, tc.tile_pool(name="wtmp", bufs=1) as wtmp, tc.tile_pool(
        name="ring", bufs=RING
    ) as ring, tc.tile_pool(name="stage", bufs=GRP_BUFS) as stage, tc.tile_pool(name="outs", bufs=1) as outs, tc.psum_pool(
        name="psum", bufs=1
    ) as psum:
        ident = const.tile([P, P], F32, name="ident")
        make_identity(nc, ident[:])
        zb = const.tile([P, 512], BF16, name="zb")
        nc.vector.memset(zb[:], 0.0)

        w0c = const.tile([P, 1280], U32, name="w0c", align_bytes=64)
        w0s = const.tile([P, 1280], U8, name="w0s", align_bytes=64)
        w1c = const.tile([P, 1536], U32, name="w1c", align_bytes=64)
        w1s = const.tile([P, 1536], U8, name="w1s", align_bytes=64)
        w2c = const.tile([P, 640], U32, name="w2c", align_bytes=64)
        w2s = const.tile([P, 640], U8, name="w2s", align_bytes=64)
        raw0 = wtmp.tile([P, 12, 384], BF16, name="raw0")
        raw1 = wtmp.tile([P, 16, 256], BF16, name="raw1")
        raw2 = wtmp.tile([P, 8, 128], BF16, name="raw2")
        grouped = {}

        def grouped_tile(which, width):
            if which not in grouped:
                grouped[which] = wtmp.tile([P, width, 4], BF16, name="gw%d" % which, tag="gw", align_bytes=64)
            return grouped[which]

        def load_w(raw, w):
            nc.sync.dma_start(
                out=raw[:].rearrange("p (a e) c -> p a (e c)", e=2),
                in_=w.rearrange("(a p e) c -> p a (e c)", p=P, e=2),
            )

        def regroup(dst, src):
            d = dst.rearrange("p (c i) t -> p c t i", i=4)
            s = src.rearrange("p t (c i) -> p c t i", i=4)
            nc.vector.tensor_copy(out=d, in_=s)

        def negate(gw, dst, src, width):
            nc.vector.tensor_scalar_mul(
                out=gw[:, dst : dst + width, :].rearrange("p c t -> p (c t)"),
                in0=gw[:, src : src + width, :].rearrange("p c t -> p (c t)"),
                scalar1=-1.0,
            )

        def quant_w(codes, scales, gw, lo, hi):
            nc.vector.quantize_mx(
                out=codes[:, lo:hi].bitcast(E4X4),
                scales=scales[:, lo:hi],
                in_=gw[:, lo:hi, :].rearrange("p c t -> p (c t)"),
            )

        def zero(codes, scales, lo, hi):
            nc.vector.memset(codes[:, lo:hi].bitcast(I32), 0)
            nc.vector.memset(scales[:, lo:hi].bitcast(I32), 0)

        def prep_w2():
            gw2 = grouped_tile(2, 384)
            regroup(gw2[:, 0:128, :], raw2[:, 4:8, :])
            regroup(gw2[:, 128:256, :], raw2[:, 0:4, :])
            negate(gw2, 256, 0, 128)
            quant_w(w2c, w2s, gw2, 0, 256)
            quant_w(w2c, w2s, gw2, 256, 384)

        w0_items = []
        for j in range(3):
            w0_items.append(lambda j=j: regroup(grouped_tile(0, 1152)[:, 384 * j : 384 * (j + 1), :], raw0[:, 4 * j : 4 * j + 4, :]))
        w0_items.append(lambda: quant_w(w0c, w0s, grouped_tile(0, 1152), 0, 1024))
        w0_items.append(lambda: quant_w(w0c, w0s, grouped_tile(0, 1152), 1024, 1152))

        w1_items = []
        for j in range(2):
            for part in range(2):
                h = 1 - part
                base = 768 * j + 256 * part
                w1_items.append(
                    lambda j=j, h=h, base=base: regroup(
                        grouped_tile(1, 1536)[:, base : base + 256, :], raw1[:, (2 * h + j) * 4 : (2 * h + j) * 4 + 4, :]
                    )
                )
            w1_items.append(lambda j=j: negate(grouped_tile(1, 1536), 768 * j + 512, 768 * j, 256))
        w1_items.append(lambda: quant_w(w1c, w1s, grouped_tile(1, 1536), 0, 1024))
        w1_items.append(lambda: quant_w(w1c, w1s, grouped_tile(1, 1536), 1024, 1536))

        moving = {}
        for j in range(3):
            moving[j] = (w0c, w0s, 384 * j)
        for j in range(2):
            moving[3 + j] = (w1c, w1s, 768 * j + 256)
            moving[5 + j] = (w1c, w1s, 768 * j)
        moving[7] = (w2c, w2s, 128)
        moving[8] = (w2c, w2s, 0)
        out_span = {"m0": (0, 384), "m1": (384, 512), "m2": (896, 256)}

        opair = []
        for j in range(NT // 2):
            opair.append(outs.tile([P, 2, OUTW], F32, name="op%d" % j))

        graw = {}
        gcodes = {}
        w0_next = [0]
        w1_next = [0]
        group = [None]
        waiting = []

        def load(gi):
            kind, c0, ncomp, t0, ntile = units[gi]
            g = ring.tile([P, ntile * ncomp * KP], BF16, name="graw", tag="graw")
            nc.sync.dma_start(
                out=g[:].rearrange("p (a k) -> p a k", a=ntile),
                in_=gv[:, t0 : t0 + ntile, c0 * KP : (c0 + ncomp) * KP],
            )
            graw[gi] = g
            if gi == W0_LOAD_AFTER:
                load_w(raw0, W0)
            if gi == W1_LOAD_AFTER:
                load_w(raw1, W1)

        def transposes(piece, turn):
            nops = len(piece)
            kind = units[piece[0][0]][0]
            grp = stage.tile([P, nops * KP], BF16, name="grp", tag="grp", align_bytes=64)
            gc = stage.tile([P, nops * P], U32, name="gc", tag="gc", bufs=CODE_BUFS, align_bytes=64)
            gs = stage.tile([P, nops * P], U8, name="gs", tag="gs", bufs=CODE_BUFS, align_bytes=64)
            gcodes[piece[0]] = (gc, gs)
            grpw = grp[:].bitcast(F32)
            nbanks = nops // 2
            who = EVAC[kind]
            done = []
            for b in range(nbanks):
                gi, o = piece[2 * b]
                words = graw[gi][:].bitcast(F32)
                tb = psum.tile([P, 4, P], F32, name="tb", tag="tb", bufs=NTB)
                for q in range(4):
                    w_lo = (2 * o + q) * P
                    nc.tensor.transpose(out=tb[:, q, :], in_=words[:, w_lo : w_lo + P], identity=ident[:])
                dst = grpw[:, b * 512 : (b + 1) * 512].rearrange("p (a e u) -> p a e u", a=2, u=2)
                src = tb[:].rearrange("p (a u) e -> p a e u", u=2)
                if who[(turn + b) % len(who)] == "V":
                    nc.vector.tensor_copy(out=dst, in_=src)
                else:
                    nc.scalar.copy(out=dst, in_=src)
                if b % 2 == 1 or b == nbanks - 1:
                    lo = (b - b % 2) * 256
                    hi = (b + 1) * 256
                    waiting.append(
                        lambda lo=lo, hi=hi, gc=gc, gs=gs, grp=grp: nc.vector.quantize_mx(
                            out=gc[:, lo:hi].bitcast(E5X4), scales=gs[:, lo:hi], in_=grp[:, 4 * lo : 4 * hi]
                        )
                    )
                if o + 2 == units[gi][2] * units[gi][4]:
                    done.append(gi)
                    if gi + RING < n:
                        load(gi + RING)
            return done

        def finish(kind, t, ob):
            col0, width = out_span[kind]
            pair = opair[t // 2]
            nc.scalar.copy(out=pair[:, t % 2, col0 : col0 + width], in_=ob[:, 0:width])
            if kind == "m0" and t >= LATE and t % 2 == 1:
                nc.sync.dma_start(out=ov[:, t - 1 : t + 1, 0:384], in_=pair[:, :, 0:384])
                nc.sync.dma_start(out=ov[:, t - 1 : t + 1, 896:1152], in_=pair[:, :, 896:1152])
            if kind == "m1":
                if t >= LATE:
                    nc.sync.dma_start(out=ov[:, t : t + 1, 384:896], in_=pair[:, t % 2 : t % 2 + 1, 384:896])
                elif t % 2 == 1:
                    nc.sync.dma_start(out=ov[:, t - 1 : t + 1, :], in_=pair[:])

        def passes(piece):
            gc, gs = gcodes[piece[0]]
            for i in range(len(piece)):
                gi, o = piece[i]
                kind, c0, ncomp, t0, ntile = units[gi]
                a = o // ncomp
                ci = o % ncomp
                if ci == 0:
                    group[0] = psum.tile([P, 512], F32, name="ob", tag="ob", bufs=NOB)
                ob = group[0]
                wc, ws, off = moving[c0 + ci]
                nc.tensor.matmul_mx(
                    out=ob[:],
                    lhsT=gc[:, i * P : (i + 1) * P].bitcast(E5X4),
                    lhsT_scale=gs[:, i * P : (i + 1) * P],
                    rhs=wc[:, off : off + 512].bitcast(E4X4),
                    rhs_scale=ws[:, off : off + 512],
                    start=(ci == 0),
                    stop=(ci == ncomp - 1),
                )
                if ci == ncomp - 1:
                    finish(kind, t0 + a, ob)

        def warm(count):
            for i in range(count):
                wb = psum.tile([P, 512], F32, name="wb", tag="ob", bufs=NOB)
                nc.tensor.matmul(out=wb[:], lhsT=zb[:, 0:P], rhs=zb[:], start=True, stop=True)

        if W2_LOAD_AFTER < 0:
            load_w(raw2, W2)
        for gi in range(RING):
            load(gi)
            if gi == W2_LOAD_AFTER:
                load_w(raw2, W2)
        zero(w2c, w2s, 384, 640)
        zero(w0c, w0s, 1152, 1280)
        prep_w2()
        warm(WARM.get(-1, 0))

        pieces = []
        for kind in ("m2", "m0", "m1"):
            stream = []
            for gi in range(n):
                if units[gi][0] == kind:
                    for o in range(units[gi][2] * units[gi][4]):
                        stream.append((gi, o))
            lo = 0
            for size in PIECES[kind]:
                pieces.append(tuple(stream[lo : lo + size]))
                lo += size
            assert lo == len(stream)

        for s in range(len(pieces) + LAG):
            done = []
            if s < len(pieces):
                done = transposes(pieces[s], s)
            warm(WARM.get(s, 0))
            if s >= LAG:
                passes(pieces[s - LAG])
            for go in waiting:
                go()
            waiting.clear()
            for gi in done:
                for i in range(W0_PREP.get(gi, 0)):
                    w0_items[w0_next[0]]()
                    w0_next[0] += 1
                for i in range(W1_PREP.get(gi, 0)):
                    w1_items[w1_next[0]]()
                    w1_next[0] += 1
